import numpy as np
import ml_dtypes


def mxq(x, axis, fmt="e4m3"):
    dtype, down = {"e4m3": (ml_dtypes.float8_e4m3fn, 7), "e5m2": (ml_dtypes.float8_e5m2, 14)}[fmt]
    v = np.moveaxis(np.asarray(x, np.float32).astype(ml_dtypes.bfloat16).astype(np.float64), axis, -1)
    blocks = v.reshape(v.shape[:-1] + (-1, 32))
    amax = np.abs(blocks).max(-1, keepdims=True)
    byte = np.maximum(np.where(amax > 0, np.frexp(amax)[1] - 1 + 127, 0) - down, 1)
    scale = np.exp2(byte - 127.0)
    codes = (blocks / scale).astype(np.float32).astype(dtype).astype(np.float64)
    return np.moveaxis((codes * scale).reshape(v.shape), -1, axis)


WIDE = False


def mx_kscale(k):
    if not WIDE:
        return np.ones(k)
    levels = np.array([10, -10, 5, -5, 0])
    a = np.random.permutation(np.resize(levels, k // 512 * 4)).reshape(k // 512, 4)
    idx = np.arange(k)
    return np.exp2(a[idx // 512, idx % 128 // 32])


BF16 = ml_dtypes.bfloat16


def bf(x):
    return np.asarray(x, np.float32).astype(BF16)


def f64(x):
    return np.asarray(x).astype(np.float64)


E2M1 = np.array([0.0, 0.5, 1.0, 1.5, 2.0, 3.0, 4.0, 6.0, -0.0, -0.5, -1.0, -1.5, -2.0, -3.0, -4.0, -6.0])


def pack_weight(w, fmt):
    k, n = w.shape
    w = f64(bf(w)).reshape(k // 32, 32, n)
    amax = np.abs(w).max(1)
    if fmt == "e4m3":
        byte = np.frexp(amax)[1] - 1 + 127 - 7
    else:
        mant, ex = np.frexp(amax / 6.0)
        byte = np.where(mant > 0.5, ex, ex - 1) + 127
    byte = np.clip(np.where(amax > 0, byte, 1), 1, 254)
    scaled = (w * np.exp2(127.0 - byte)[:, None, :]).reshape(k, n).astype(np.float32)
    by_word = np.ascontiguousarray(scaled.reshape(k // 512, 128, 4, n).transpose(0, 1, 3, 2))
    if fmt == "e4m3":
        words = by_word.astype(ml_dtypes.float8_e4m3fn).view(np.uint8)
    else:
        c = by_word.astype(ml_dtypes.float4_e2m1fn).view(np.uint8) & 0xF
        words = c[..., 0::2] | (c[..., 1::2] << 4)
    return np.ascontiguousarray(words), np.ascontiguousarray(byte.astype(np.uint8).reshape(k // 512, 16, n))


def unpack_weight(words, scales, fmt):
    g, p, n, _ = words.shape
    if fmt == "e4m3":
        vals = np.ascontiguousarray(words).view(ml_dtypes.float8_e4m3fn).astype(np.float64)
    else:
        nib = np.empty((g, p, n, 4), np.uint8)
        nib[..., 0::2] = words & 0xF
        nib[..., 1::2] = words >> 4
        vals = E2M1[nib]
    vals = vals * np.repeat(np.exp2(scales.astype(np.float64) - 127.0), 8, axis=1)[..., None]
    return vals.transpose(0, 1, 3, 2).reshape(g * 512, n)


P, N, Z, H1, H2, C = 8, 256, 16, 512, 2048, 256
EPS = 1e-5


def batch_norm(h, gamma, beta):
    mu = h.mean(axis=1, keepdims=True)
    var = h.var(axis=1, keepdims=True)
    return (h - mu) * (1.0 / np.sqrt(var + EPS)) * gamma[:, None, :] + beta[:, None, :]


def setup_inputs():
    r = np.random.standard_normal
    t = mx_kscale(H1)
    sd = np.where(np.random.random((P, 1, H1)) < 0.25, np.sqrt(EPS), 1.0)
    h6_pre = bf((r((P, N, H1)) + 0.5 * r((P, 1, H1))) * sd)
    g6 = bf((1.0 + 0.1 * r((P, H1))) * t)
    be6 = bf(0.3 * r((P, H1)) * t)
    w7 = r((P, H2, H1)) / np.sqrt(H1) / t
    b7 = bf(0.3 * r((P, H2)))
    cat = np.ascontiguousarray(w7.swapaxes(1, 2)).reshape(-1, H2)
    words, scales = pack_weight(cat, "e4m3")
    return {"h6_pre": h6_pre,
            "g6": g6,
            "be6": be6,
            "W7_words": words,
            "W7_scales": scales,
            "b7": b7}


def reference(h6_pre, g6, be6, W7_words, W7_scales, b7):
    a = np.maximum(batch_norm(f64(h6_pre), f64(g6), f64(be6)), 0.0)
    y = mxq(a, 2, "e4m3") @ unpack_weight(W7_words, W7_scales, "e4m3").reshape(P, H1, H2)
    return y + f64(b7)[:, None, :]

@@ -1,0 +1,180 @@
+from contextlib import ExitStack
+
+import concourse.mybir as mybir
+from concourse.masks import make_identity
+
+FP8X4 = mybir.dt.float8_e4m3fn_x4
+BF16 = mybir.dt.bfloat16
+F32 = mybir.dt.float32
+I32 = mybir.dt.int32
+U32 = mybir.dt.uint32
+U8 = mybir.dt.uint8
+ACT = mybir.ActivationFunctionType
+ALU = mybir.AluOpType
+
+BLOCKS = 8
+ROWS = 256
+K = 512
+COLS = 2048
+EPS = 1e-5
+
+P = 128
+PACK = 4
+ROW_TILES = ROWS // P
+N_TILE = 512
+COL_TILES = COLS // N_TILE
+SHARED = 4
+QUADRANT = 32
+SPREAD = 1024
+
+FLOPS = 2 * BLOCKS * ROWS * K * COLS
+
+
+def tile_decoder_pa_e_kernel(tc, h6_pre, g6, be6, W7_words, W7_scales, b7, out):
+    nc = tc.nc
+    with ExitStack() as stack:
+        keep = stack.enter_context(tc.tile_pool(name="keep", bufs=1))
+        small = stack.enter_context(tc.tile_pool(name="small", bufs=2))
+        work = stack.enter_context(tc.tile_pool(name="work", bufs=2))
+        results = stack.enter_context(tc.tile_pool(name="results", bufs=4))
+        psum_h = stack.enter_context(tc.psum_pool(name="psum_h", bufs=2))
+        psum_bias = stack.enter_context(tc.psum_pool(name="psum_bias", bufs=2))
+        psum_acc = stack.enter_context(tc.psum_pool(name="psum_acc", bufs=4))
+
+        h_rows = keep.tile([P, BLOCKS, ROW_TILES, K], BF16)
+        w_words = keep.tile([P, BLOCKS, COLS], U32, align_bytes=64)
+        w_planes = keep.tile([P, BLOCKS // SHARED, COLS], U8, align_bytes=64)
+        a_words = keep.tile([P, BLOCKS, ROWS], U32, align_bytes=64)
+        a_planes = keep.tile([P, BLOCKS, ROWS], U8, align_bytes=64)
+        bias_all = keep.tile([P, BLOCKS, COLS], BF16)
+        vectors = keep.tile([P, K], BF16)
+        bias_rows = keep.tile([P, P], BF16)
+        bias_cols = keep.tile([P, P], BF16)
+        gain_shift = keep.tile([P, 2 * BLOCKS, PACK], F32)
+        identity = keep.tile([P, P], BF16)
+        one = keep.tile([P, 1], F32)
+        warm = keep.tile([P, 1], F32)
+
+        nc.vector.memset(w_planes[:].bitcast(I32), 0)
+        nc.vector.memset(vectors[:], 0.0)
+        nc.vector.memset(one[:], 1.0)
+        make_identity(nc, identity[:])
+        nc.scalar.activation(out=warm[:], in_=one[:], func=ACT.Sqrt)
+
+        def load_h(e):
+            nc.sync.dma_start(out=h_rows[:, e, :, :], in_=h6_pre[e].rearrange("(q r) k -> q r k", r=ROW_TILES))
+
+        def load_w(e):
+            nc.sync.dma_start(
+                out=w_words[:, e, :].bitcast(I32),
+                in_=W7_words[e].rearrange("p n t -> p (n t)").bitcast(I32),
+            )
+
+        load_h(0)
+        for group in range(BLOCKS // SHARED):
+            for quadrant in range(P // QUADRANT):
+                first = QUADRANT * quadrant
+                nc.sync.dma_start(
+                    out=w_planes[first : first + 4 * SHARED, group, :].bitcast(I32),
+                    in_=W7_scales[SHARED * group : SHARED * (group + 1), 4 * quadrant : 4 * quadrant + 4, :].bitcast(I32),
+                )
+        nc.sync.dma_start(out=vectors[0:BLOCKS, :], in_=g6[:, :])
+        nc.sync.dma_start(out=vectors[BLOCKS : 2 * BLOCKS, :], in_=be6[:, :])
+        nc.sync.dma_start(out=bias_rows[:], in_=b7.rearrange("e (c j) -> (e c) j", j=P))
+        for e in range(BLOCKS):
+            load_w(e)
+            if e + 1 < BLOCKS:
+                load_h(e + 1)
+
+        vectors_t = psum_h.tile([P, PACK, P], BF16, tag="h_t")
+        for t in range(PACK):
+            nc.tensor.transpose(vectors_t[:, t, :], vectors[:, t:K:PACK], identity[:])
+        nc.vector.tensor_copy(out=gain_shift[:], in_=vectors_t[:, :, 0 : 2 * BLOCKS].rearrange("p t v -> p v t"))
+        bias_t = psum_bias.tile([P, P], BF16, tag="spread")
+        nc.tensor.transpose(bias_t[:], bias_rows[:], identity[:])
+        nc.vector.tensor_copy(out=bias_cols[:], in_=bias_t[:])
+
+        def normalise(e):
+            h_t = psum_h.tile([P, PACK, ROWS], BF16, tag="h_t")
+            for r in range(ROW_TILES):
+                for t in range(PACK):
+                    nc.tensor.transpose(h_t[:, t, P * r : P * (r + 1)], h_rows[:, e, r, t:K:PACK], identity[:])
+
+            stats = small.tile([P, PACK, 6], F32)
+            mean_var = small.tile([P, PACK, 2], F32)
+            for t in range(PACK):
+                nc.vector.bn_stats(out=stats[:, t, :], in_=h_t[:, t, :])
+            for t in range(PACK):
+                nc.vector.bn_aggr(out=mean_var[:, t, :], in_=stats[:, t, :])
+
+            var_eps = small.tile([P, PACK], F32)
+            std = small.tile([P, PACK], F32)
+            rstd = small.tile([P, PACK], F32)
+            scale = small.tile([P, PACK], F32)
+            mean_scaled = small.tile([P, PACK], F32)
+            shift = small.tile([P, PACK], F32)
+            nc.vector.tensor_scalar_add(out=var_eps[:], in0=mean_var[:, :, 1], scalar1=EPS)
+            nc.scalar.activation(out=std[:], in_=var_eps[:], func=ACT.Sqrt)
+            nc.vector.reciprocal(out=rstd[:], in_=std[:])
+            nc.vector.tensor_tensor(out=scale[:], in0=gain_shift[:, e, :], in1=rstd[:], op=ALU.mult)
+            nc.vector.tensor_tensor(out=mean_scaled[:], in0=mean_var[:, :, 0], in1=scale[:], op=ALU.mult)
+            nc.vector.tensor_tensor(out=shift[:], in0=gain_shift[:, BLOCKS + e, :], in1=mean_scaled[:], op=ALU.subtract)
+
+            a_t = work.tile([P, PACK, ROWS], BF16)
+            for t in range(PACK):
+                nc.scalar.activation(
+                    out=a_t[:, t, :], in_=h_t[:, t, :], func=ACT.Relu, scale=scale[:, t : t + 1], bias=shift[:, t : t + 1]
+                )
+            grouped = work.tile([P, ROWS, PACK], BF16, align_bytes=64)
+            nc.vector.tensor_copy(out=grouped[:], in_=a_t[:].rearrange("p t n -> p n t"))
+            nc.vector.quantize_mx(
+                out=a_words[:, e, :].bitcast(FP8X4),
+                scales=a_planes[:, e, :],
+                in_=grouped[:].rearrange("p n t -> p (n t)"),
+            )
+
+        def spread_bias(e):
+            for half in range(COLS // SPREAD):
+                spread = psum_bias.tile([P, SPREAD], BF16, tag="spread")
+                for i in range(SPREAD // P):
+                    chunk = (COLS // P) * e + (SPREAD // P) * half + i
+                    nc.tensor.transpose(
+                        spread[:, P * i : P * (i + 1)], bias_cols[:, chunk : chunk + 1].to_broadcast([P, P]), identity[:]
+                    )
+                nc.scalar.copy(out=bias_all[:, e, SPREAD * half : SPREAD * (half + 1)], in_=spread[:])
+
+        def multiply(e):
+            plane_start = 4 * (e % SHARED)
+            by_vector = results.tile([P, COLS], F32)
+            by_scalar = results.tile([P, COLS], F32)
+            for c in range(COL_TILES):
+                cols = slice(N_TILE * c, N_TILE * (c + 1))
+                for r in (1, 0):
+                    acc = psum_acc.tile([P, N_TILE], F32)
+                    nc.tensor.matmul_mx(
+                        out=acc[:],
+                        lhsT=a_words[:, e, P * r : P * (r + 1)].bitcast(FP8X4),
+                        lhsT_scale=a_planes[:, e, P * r : P * (r + 1)],
+                        rhs=w_words[:, e, cols].bitcast(FP8X4),
+                        rhs_scale=w_planes[plane_start:P, e // SHARED, cols],
+                        start=True,
+                        stop=True,
+                    )
+                    if r == 0:
+                        nc.vector.tensor_tensor(out=by_vector[:, cols], in0=acc[:], in1=bias_all[:, e, cols], op=ALU.add)
+                    else:
+                        nc.scalar.copy(out=by_scalar[:, cols], in_=acc[:])
+                        nc.gpsimd.tensor_tensor(
+                            out=by_scalar[:, cols], in0=by_scalar[:, cols], in1=bias_all[:, e, cols], op=ALU.add
+                        )
+            out_rows = out[e].rearrange("(q r) j -> q r j", r=ROW_TILES)
+            nc.sync.dma_start(out=out_rows[:, 0, :], in_=by_vector[:])
+            nc.sync.dma_start(out=out_rows[:, 1, :], in_=by_scalar[:])
+
+        normalise(0)
+        spread_bias(0)
+        for e in range(BLOCKS):
+            if e + 1 < BLOCKS:
+                normalise(e + 1)
+                spread_bias(e + 1)
+            multiply(e)

@@ -26,6 +26,7 @@ COL_TILES = COLS // N_TILE
 SHARED = 4
 QUADRANT = 32
 SPREAD = 1024
+DETOUR_EVERY = 4
 
 FLOPS = 2 * BLOCKS * ROWS * K * COLS
 
@@ -145,11 +146,10 @@ def tile_decoder_pa_e_kernel(tc, h6_pre, g6, be6, W7_words, W7_scales, b7, out):
 
         def multiply(e):
             plane_start = 4 * (e % SHARED)
-            by_vector = results.tile([P, COLS], F32)
-            by_scalar = results.tile([P, COLS], F32)
+            result = [results.tile([P, COLS], F32, name="result%d" % r) for r in range(ROW_TILES)]
             for c in range(COL_TILES):
                 cols = slice(N_TILE * c, N_TILE * (c + 1))
-                for r in (1, 0):
+                for r in range(ROW_TILES):
                     acc = psum_acc.tile([P, N_TILE], F32)
                     nc.tensor.matmul_mx(
                         out=acc[:],
@@ -160,16 +160,15 @@ def tile_decoder_pa_e_kernel(tc, h6_pre, g6, be6, W7_words, W7_scales, b7, out):
                         start=True,
                         stop=True,
                     )
-                    if r == 0:
-                        nc.vector.tensor_tensor(out=by_vector[:, cols], in0=acc[:], in1=bias_all[:, e, cols], op=ALU.add)
+                    target = result[r][:, cols]
+                    if (ROW_TILES * c + r) % DETOUR_EVERY == DETOUR_EVERY - 1:
+                        nc.scalar.copy(out=target, in_=acc[:])
+                        nc.gpsimd.tensor_tensor(out=target, in0=target, in1=bias_all[:, e, cols], op=ALU.add)
                     else:
-                        nc.scalar.copy(out=by_scalar[:, cols], in_=acc[:])
-                        nc.gpsimd.tensor_tensor(
-                            out=by_scalar[:, cols], in0=by_scalar[:, cols], in1=bias_all[:, e, cols], op=ALU.add
-                        )
+                        nc.vector.tensor_tensor(out=target, in0=acc[:], in1=bias_all[:, e, cols], op=ALU.add)
             out_rows = out[e].rearrange("(q r) j -> q r j", r=ROW_TILES)
-            nc.sync.dma_start(out=out_rows[:, 0, :], in_=by_vector[:])
-            nc.sync.dma_start(out=out_rows[:, 1, :], in_=by_scalar[:])
+            for r in range(ROW_TILES):
+                nc.sync.dma_start(out=out_rows[:, r, :], in_=result[r][:])
 
         normalise(0)
         spread_bias(0)

@@ -20,12 +20,14 @@ EPS = 1e-5
 
 P = 128
 PACK = 4
+PAIR = 2
 ROW_TILES = ROWS // P
 N_TILE = 512
 COL_TILES = COLS // N_TILE
 SHARED = 4
 QUADRANT = 32
-SPREAD = 1024
+SPREAD = PAIR * N_TILE
+CHUNK = PAIR * P
 DETOUR_EVERY = 4
 
 FLOPS = 2 * BLOCKS * ROWS * K * COLS
@@ -49,15 +51,16 @@ def tile_decoder_pa_e_kernel(tc, h6_pre, g6, be6, W7_words, W7_scales, b7, out):
         a_planes = keep.tile([P, BLOCKS, ROWS], U8, align_bytes=64)
         bias_all = keep.tile([P, BLOCKS, COLS], BF16)
         vectors = keep.tile([P, K], BF16)
-        bias_rows = keep.tile([P, P], BF16)
-        bias_cols = keep.tile([P, P], BF16)
+        bias_rows = keep.tile([P, CHUNK], BF16)
+        bias_cols = keep.tile([P, P], F32)
         gain_shift = keep.tile([P, 2 * BLOCKS, PACK], F32)
-        identity = keep.tile([P, P], BF16)
+        identity = keep.tile([P, P], F32)
         one = keep.tile([P, 1], F32)
         warm = keep.tile([P, 1], F32)
 
         nc.vector.memset(w_planes[:].bitcast(I32), 0)
         nc.vector.memset(vectors[:], 0.0)
+        nc.vector.memset(bias_rows[:], 0.0)
         nc.vector.memset(one[:], 1.0)
         make_identity(nc, identity[:])
         nc.scalar.activation(out=warm[:], in_=one[:], func=ACT.Sqrt)
@@ -81,30 +84,39 @@ def tile_decoder_pa_e_kernel(tc, h6_pre, g6, be6, W7_words, W7_scales, b7, out):
                 )
         nc.sync.dma_start(out=vectors[0:BLOCKS, :], in_=g6[:, :])
         nc.sync.dma_start(out=vectors[BLOCKS : 2 * BLOCKS, :], in_=be6[:, :])
-        nc.sync.dma_start(out=bias_rows[:], in_=b7.rearrange("e (c j) -> (e c) j", j=P))
+        nc.sync.dma_start(out=bias_rows[0 : BLOCKS * COLS // CHUNK, :], in_=b7.rearrange("e (c j) -> (e c) j", j=CHUNK))
         for e in range(BLOCKS):
             load_w(e)
             if e + 1 < BLOCKS:
                 load_h(e + 1)
 
-        vectors_t = psum_h.tile([P, PACK, P], BF16, tag="h_t")
-        for t in range(PACK):
-            nc.tensor.transpose(vectors_t[:, t, :], vectors[:, t:K:PACK], identity[:])
-        nc.vector.tensor_copy(out=gain_shift[:], in_=vectors_t[:, :, 0 : 2 * BLOCKS].rearrange("p t v -> p v t"))
-        bias_t = psum_bias.tile([P, P], BF16, tag="spread")
-        nc.tensor.transpose(bias_t[:], bias_rows[:], identity[:])
+        vectors_t = psum_h.tile([P, PACK // PAIR, P], F32, tag="h_t")
+        for u in range(PACK // PAIR):
+            nc.tensor.transpose(vectors_t[:, u, :], vectors[:].bitcast(F32)[:, u : K // PAIR : PACK // PAIR], identity[:])
+        nc.vector.tensor_copy(
+            out=gain_shift[:].rearrange("p v (u i) -> p v u i", i=PAIR),
+            in_=vectors_t[:].bitcast(BF16).rearrange("p u (v i) -> p v u i", i=PAIR)[:, 0 : 2 * BLOCKS, :, :],
+        )
+        bias_t = psum_bias.tile([P, P], F32, tag="spread")
+        nc.tensor.transpose(bias_t[:], bias_rows[:].bitcast(F32), identity[:])
         nc.vector.tensor_copy(out=bias_cols[:], in_=bias_t[:])
 
         def normalise(e):
-            h_t = psum_h.tile([P, PACK, ROWS], BF16, tag="h_t")
+            h_t = psum_h.tile([P, PACK // PAIR, ROWS], F32, tag="h_t")
             for r in range(ROW_TILES):
-                for t in range(PACK):
-                    nc.tensor.transpose(h_t[:, t, P * r : P * (r + 1)], h_rows[:, e, r, t:K:PACK], identity[:])
+                for u in range(PACK // PAIR):
+                    nc.tensor.transpose(
+                        h_t[:, u, P * r : P * (r + 1)],
+                        h_rows[:, e, r, :].bitcast(F32)[:, u : K // PAIR : PACK // PAIR],
+                        identity[:],
+                    )
+            pairs = h_t[:].bitcast(BF16).rearrange("p u (n i) -> p u n i", i=PAIR)
+            planes = [pairs[:, t // PAIR, :, t % PAIR] for t in range(PACK)]
 
             stats = small.tile([P, PACK, 6], F32)
             mean_var = small.tile([P, PACK, 2], F32)
             for t in range(PACK):
-                nc.vector.bn_stats(out=stats[:, t, :], in_=h_t[:, t, :])
+                nc.vector.bn_stats(out=stats[:, t, :], in_=planes[t])
             for t in range(PACK):
                 nc.vector.bn_aggr(out=mean_var[:, t, :], in_=stats[:, t, :])
 
@@ -124,7 +136,7 @@ def tile_decoder_pa_e_kernel(tc, h6_pre, g6, be6, W7_words, W7_scales, b7, out):
             a_t = work.tile([P, PACK, ROWS], BF16)
             for t in range(PACK):
                 nc.scalar.activation(
-                    out=a_t[:, t, :], in_=h_t[:, t, :], func=ACT.Relu, scale=scale[:, t : t + 1], bias=shift[:, t : t + 1]
+                    out=a_t[:, t, :], in_=planes[t], func=ACT.Relu, scale=scale[:, t : t + 1], bias=shift[:, t : t + 1]
                 )
             grouped = work.tile([P, ROWS, PACK], BF16, align_bytes=64)
             nc.vector.tensor_copy(out=grouped[:], in_=a_t[:].rearrange("p t n -> p n t"))
@@ -136,13 +148,13 @@ def tile_decoder_pa_e_kernel(tc, h6_pre, g6, be6, W7_words, W7_scales, b7, out):
 
         def spread_bias(e):
             for half in range(COLS // SPREAD):
-                spread = psum_bias.tile([P, SPREAD], BF16, tag="spread")
-                for i in range(SPREAD // P):
-                    chunk = (COLS // P) * e + (SPREAD // P) * half + i
+                spread = psum_bias.tile([P, N_TILE], F32, tag="spread")
+                for i in range(SPREAD // CHUNK):
+                    chunk = (COLS // CHUNK) * e + (SPREAD // CHUNK) * half + i
                     nc.tensor.transpose(
                         spread[:, P * i : P * (i + 1)], bias_cols[:, chunk : chunk + 1].to_broadcast([P, P]), identity[:]
                     )
-                nc.scalar.copy(out=bias_all[:, e, SPREAD * half : SPREAD * (half + 1)], in_=spread[:])
+                nc.scalar.copy(out=bias_all[:, e, SPREAD * half : SPREAD * (half + 1)].bitcast(F32), in_=spread[:])
 
         def multiply(e):
             plane_start = 4 * (e % SHARED)

@@ -23,12 +23,12 @@ PACK = 4
 PAIR = 2
 ROW_TILES = ROWS // P
 N_TILE = 512
-COL_TILES = COLS // N_TILE
+HALF = COLS // 2
 SHARED = 4
 QUADRANT = 32
-SPREAD = PAIR * N_TILE
 CHUNK = PAIR * P
 DETOUR_EVERY = 4
+AHEAD = 2
 
 FLOPS = 2 * BLOCKS * ROWS * K * COLS
 
@@ -39,10 +39,11 @@ def tile_decoder_pa_e_kernel(tc, h6_pre, g6, be6, W7_words, W7_scales, b7, out):
         keep = stack.enter_context(tc.tile_pool(name="keep", bufs=1))
         small = stack.enter_context(tc.tile_pool(name="small", bufs=2))
         work = stack.enter_context(tc.tile_pool(name="work", bufs=2))
-        results = stack.enter_context(tc.tile_pool(name="results", bufs=4))
+        results = stack.enter_context(tc.tile_pool(name="results", bufs=8))
         psum_h = stack.enter_context(tc.psum_pool(name="psum_h", bufs=2))
         psum_bias = stack.enter_context(tc.psum_pool(name="psum_bias", bufs=2))
         psum_acc = stack.enter_context(tc.psum_pool(name="psum_acc", bufs=4))
+        stack.enter_context(tc.manual_schedule())
 
         h_rows = keep.tile([P, BLOCKS, ROW_TILES, K], BF16)
         w_words = keep.tile([P, BLOCKS, COLS], U32, align_bytes=64)
@@ -58,9 +59,9 @@ def tile_decoder_pa_e_kernel(tc, h6_pre, g6, be6, W7_words, W7_scales, b7, out):
         one = keep.tile([P, 1], F32)
         warm = keep.tile([P, 1], F32)
 
-        nc.vector.memset(w_planes[:].bitcast(I32), 0)
         nc.vector.memset(vectors[:], 0.0)
         nc.vector.memset(bias_rows[:], 0.0)
+        nc.vector.memset(w_planes[:].bitcast(I32), 0)
         nc.vector.memset(one[:], 1.0)
         make_identity(nc, identity[:])
         nc.scalar.activation(out=warm[:], in_=one[:], func=ACT.Sqrt)
@@ -75,6 +76,10 @@ def tile_decoder_pa_e_kernel(tc, h6_pre, g6, be6, W7_words, W7_scales, b7, out):
             )
 
         load_h(0)
+        nc.sync.dma_start(out=vectors[0:BLOCKS, :], in_=g6[:, :])
+        nc.sync.dma_start(out=vectors[BLOCKS : 2 * BLOCKS, :], in_=be6[:, :])
+        nc.sync.dma_start(out=bias_rows[0 : BLOCKS * COLS // CHUNK, :], in_=b7.rearrange("e (c j) -> (e c) j", j=CHUNK))
+        load_h(1)
         for group in range(BLOCKS // SHARED):
             for quadrant in range(P // QUADRANT):
                 first = QUADRANT * quadrant
@@ -82,26 +87,18 @@ def tile_decoder_pa_e_kernel(tc, h6_pre, g6, be6, W7_words, W7_scales, b7, out):
                     out=w_planes[first : first + 4 * SHARED, group, :].bitcast(I32),
                     in_=W7_scales[SHARED * group : SHARED * (group + 1), 4 * quadrant : 4 * quadrant + 4, :].bitcast(I32),
                 )
-        nc.sync.dma_start(out=vectors[0:BLOCKS, :], in_=g6[:, :])
-        nc.sync.dma_start(out=vectors[BLOCKS : 2 * BLOCKS, :], in_=be6[:, :])
-        nc.sync.dma_start(out=bias_rows[0 : BLOCKS * COLS // CHUNK, :], in_=b7.rearrange("e (c j) -> (e c) j", j=CHUNK))
         for e in range(BLOCKS):
             load_w(e)
-            if e + 1 < BLOCKS:
-                load_h(e + 1)
+            if e + AHEAD < BLOCKS:
+                load_h(e + AHEAD)
 
-        vectors_t = psum_h.tile([P, PACK // PAIR, P], F32, tag="h_t")
-        for u in range(PACK // PAIR):
-            nc.tensor.transpose(vectors_t[:, u, :], vectors[:].bitcast(F32)[:, u : K // PAIR : PACK // PAIR], identity[:])
-        nc.vector.tensor_copy(
-            out=gain_shift[:].rearrange("p v (u i) -> p v u i", i=PAIR),
-            in_=vectors_t[:].bitcast(BF16).rearrange("p u (v i) -> p v u i", i=PAIR)[:, 0 : 2 * BLOCKS, :, :],
-        )
-        bias_t = psum_bias.tile([P, P], F32, tag="spread")
-        nc.tensor.transpose(bias_t[:], bias_rows[:].bitcast(F32), identity[:])
-        nc.vector.tensor_copy(out=bias_cols[:], in_=bias_t[:])
+        h_planes = {}
+        mean_vars = {}
+        stds = {}
+        scale_shifts = {}
+        a_ts = {}
 
-        def normalise(e):
+        def transpose_h(e):
             h_t = psum_h.tile([P, PACK // PAIR, ROWS], F32, tag="h_t")
             for r in range(ROW_TILES):
                 for u in range(PACK // PAIR):
@@ -111,35 +108,59 @@ def tile_decoder_pa_e_kernel(tc, h6_pre, g6, be6, W7_words, W7_scales, b7, out):
                         identity[:],
                     )
             pairs = h_t[:].bitcast(BF16).rearrange("p u (n i) -> p u n i", i=PAIR)
-            planes = [pairs[:, t // PAIR, :, t % PAIR] for t in range(PACK)]
+            h_planes[e] = [pairs[:, t // PAIR, :, t % PAIR] for t in range(PACK)]
 
+        def transpose_vectors():
+            vectors_t = psum_bias.tile([P, PACK // PAIR, P], F32, tag="spread")
+            for u in range(PACK // PAIR):
+                nc.tensor.transpose(
+                    vectors_t[:, u, :], vectors[:].bitcast(F32)[:, u : K // PAIR : PACK // PAIR], identity[:]
+                )
+            nc.vector.tensor_copy(
+                out=gain_shift[:].rearrange("p v (u i) -> p v u i", i=PAIR),
+                in_=vectors_t[:].bitcast(BF16).rearrange("p u (v i) -> p v u i", i=PAIR)[:, 0 : 2 * BLOCKS, :, :],
+            )
+            bias_t = psum_bias.tile([P, P], F32, tag="spread")
+            nc.tensor.transpose(bias_t[:], bias_rows[:].bitcast(F32), identity[:])
+            nc.vector.tensor_copy(out=bias_cols[:], in_=bias_t[:])
+
+        def statistics(e):
             stats = small.tile([P, PACK, 6], F32)
             mean_var = small.tile([P, PACK, 2], F32)
-            for t in range(PACK):
-                nc.vector.bn_stats(out=stats[:, t, :], in_=planes[t])
-            for t in range(PACK):
-                nc.vector.bn_aggr(out=mean_var[:, t, :], in_=stats[:, t, :])
-
             var_eps = small.tile([P, PACK], F32)
             std = small.tile([P, PACK], F32)
+            for t in range(PACK):
+                nc.vector.bn_stats(out=stats[:, t, :], in_=h_planes[e][t])
+            for t in range(PACK):
+                nc.vector.bn_aggr(out=mean_var[:, t, :], in_=stats[:, t, :])
+            nc.vector.tensor_scalar_add(out=var_eps[:], in0=mean_var[:, :, 1], scalar1=EPS)
+            nc.scalar.activation(out=std[:], in_=var_eps[:], func=ACT.Sqrt)
+            mean_vars[e] = mean_var
+            stds[e] = std
+
+        def gain_and_shift(e):
             rstd = small.tile([P, PACK], F32)
             scale = small.tile([P, PACK], F32)
             mean_scaled = small.tile([P, PACK], F32)
             shift = small.tile([P, PACK], F32)
-            nc.vector.tensor_scalar_add(out=var_eps[:], in0=mean_var[:, :, 1], scalar1=EPS)
-            nc.scalar.activation(out=std[:], in_=var_eps[:], func=ACT.Sqrt)
-            nc.vector.reciprocal(out=rstd[:], in_=std[:])
+            nc.vector.reciprocal(out=rstd[:], in_=stds[e][:])
             nc.vector.tensor_tensor(out=scale[:], in0=gain_shift[:, e, :], in1=rstd[:], op=ALU.mult)
-            nc.vector.tensor_tensor(out=mean_scaled[:], in0=mean_var[:, :, 0], in1=scale[:], op=ALU.mult)
+            nc.vector.tensor_tensor(out=mean_scaled[:], in0=mean_vars[e][:, :, 0], in1=scale[:], op=ALU.mult)
             nc.vector.tensor_tensor(out=shift[:], in0=gain_shift[:, BLOCKS + e, :], in1=mean_scaled[:], op=ALU.subtract)
+            scale_shifts[e] = (scale, shift)
 
+        def norm_and_relu(e):
+            scale, shift = scale_shifts[e]
             a_t = work.tile([P, PACK, ROWS], BF16)
             for t in range(PACK):
                 nc.scalar.activation(
-                    out=a_t[:, t, :], in_=planes[t], func=ACT.Relu, scale=scale[:, t : t + 1], bias=shift[:, t : t + 1]
+                    out=a_t[:, t, :], in_=h_planes[e][t], func=ACT.Relu, scale=scale[:, t : t + 1], bias=shift[:, t : t + 1]
                 )
+            a_ts[e] = a_t
+
+        def quantise(e):
             grouped = work.tile([P, ROWS, PACK], BF16, align_bytes=64)
-            nc.vector.tensor_copy(out=grouped[:], in_=a_t[:].rearrange("p t n -> p n t"))
+            nc.vector.tensor_copy(out=grouped[:], in_=a_ts[e][:].rearrange("p t n -> p n t"))
             nc.vector.quantize_mx(
                 out=a_words[:, e, :].bitcast(FP8X4),
                 scales=a_planes[:, e, :],
@@ -147,20 +168,20 @@ def tile_decoder_pa_e_kernel(tc, h6_pre, g6, be6, W7_words, W7_scales, b7, out):
             )
 
         def spread_bias(e):
-            for half in range(COLS // SPREAD):
+            for half in range(COLS // HALF):
                 spread = psum_bias.tile([P, N_TILE], F32, tag="spread")
-                for i in range(SPREAD // CHUNK):
-                    chunk = (COLS // CHUNK) * e + (SPREAD // CHUNK) * half + i
+                for i in range(HALF // CHUNK):
+                    chunk = (COLS // CHUNK) * e + (HALF // CHUNK) * half + i
                     nc.tensor.transpose(
                         spread[:, P * i : P * (i + 1)], bias_cols[:, chunk : chunk + 1].to_broadcast([P, P]), identity[:]
                     )
-                nc.scalar.copy(out=bias_all[:, e, SPREAD * half : SPREAD * (half + 1)].bitcast(F32), in_=spread[:])
+                nc.scalar.copy(out=bias_all[:, e, HALF * half : HALF * (half + 1)].bitcast(F32), in_=spread[:])
 
-        def multiply(e):
+        def multiply(e, half):
             plane_start = 4 * (e % SHARED)
-            result = [results.tile([P, COLS], F32, name="result%d" % r) for r in range(ROW_TILES)]
-            for c in range(COL_TILES):
-                cols = slice(N_TILE * c, N_TILE * (c + 1))
+            result = results.tile([P, ROW_TILES, HALF], F32)
+            for c in range(HALF // N_TILE):
+                cols = slice(HALF * half + N_TILE * c, HALF * half + N_TILE * (c + 1))
                 for r in range(ROW_TILES):
                     acc = psum_acc.tile([P, N_TILE], F32)
                     nc.tensor.matmul_mx(
@@ -172,20 +193,33 @@ def tile_decoder_pa_e_kernel(tc, h6_pre, g6, be6, W7_words, W7_scales, b7, out):
                         start=True,
                         stop=True,
                     )
-                    target = result[r][:, cols]
+                    target = result[:, r, N_TILE * c : N_TILE * (c + 1)]
                     if (ROW_TILES * c + r) % DETOUR_EVERY == DETOUR_EVERY - 1:
                         nc.scalar.copy(out=target, in_=acc[:])
                         nc.gpsimd.tensor_tensor(out=target, in0=target, in1=bias_all[:, e, cols], op=ALU.add)
                     else:
                         nc.vector.tensor_tensor(out=target, in0=acc[:], in1=bias_all[:, e, cols], op=ALU.add)
-            out_rows = out[e].rearrange("(q r) j -> q r j", r=ROW_TILES)
-            for r in range(ROW_TILES):
-                nc.sync.dma_start(out=out_rows[:, r, :], in_=result[r][:])
+            nc.sync.dma_start(
+                out=out[e].rearrange("(q r) j -> q r j", r=ROW_TILES)[:, :, HALF * half : HALF * (half + 1)], in_=result[:]
+            )
 
-        normalise(0)
-        spread_bias(0)
-        for e in range(BLOCKS):
-            if e + 1 < BLOCKS:
-                normalise(e + 1)
-                spread_bias(e + 1)
-            multiply(e)
+        for i in range(-AHEAD, BLOCKS):
+            started = i + AHEAD
+            if started < BLOCKS:
+                transpose_h(started)
+            if started == 0:
+                transpose_vectors()
+            if 0 <= i + 1 < BLOCKS:
+                spread_bias(i + 1)
+            if started < BLOCKS:
+                statistics(started)
+            if 0 <= i + 1 < BLOCKS:
+                quantise(i + 1)
+            if i >= 0:
+                multiply(i, 0)
+            if started < BLOCKS:
+                gain_and_shift(started)
+            if i >= 0:
+                multiply(i, 1)
+            if started < BLOCKS:
+                norm_and_relu(started)

@@ -27,7 +27,6 @@ HALF = COLS // 2
 SHARED = 4
 QUADRANT = 32
 CHUNK = PAIR * P
-DETOUR_EVERY = 4
 AHEAD = 2
 
 FLOPS = 2 * BLOCKS * ROWS * K * COLS
@@ -39,7 +38,7 @@ def tile_decoder_pa_e_kernel(tc, h6_pre, g6, be6, W7_words, W7_scales, b7, out):
         keep = stack.enter_context(tc.tile_pool(name="keep", bufs=1))
         small = stack.enter_context(tc.tile_pool(name="small", bufs=2))
         work = stack.enter_context(tc.tile_pool(name="work", bufs=2))
-        results = stack.enter_context(tc.tile_pool(name="results", bufs=8))
+        results = stack.enter_context(tc.tile_pool(name="results", bufs=4))
         psum_h = stack.enter_context(tc.psum_pool(name="psum_h", bufs=2))
         psum_bias = stack.enter_context(tc.psum_pool(name="psum_bias", bufs=2))
         psum_acc = stack.enter_context(tc.psum_pool(name="psum_acc", bufs=4))
@@ -94,6 +93,7 @@ def tile_decoder_pa_e_kernel(tc, h6_pre, g6, be6, W7_words, W7_scales, b7, out):
 
         h_planes = {}
         mean_vars = {}
+        var_epss = {}
         stds = {}
         scale_shifts = {}
         a_ts = {}
@@ -128,14 +128,17 @@ def tile_decoder_pa_e_kernel(tc, h6_pre, g6, be6, W7_words, W7_scales, b7, out):
             stats = small.tile([P, PACK, 6], F32)
             mean_var = small.tile([P, PACK, 2], F32)
             var_eps = small.tile([P, PACK], F32)
-            std = small.tile([P, PACK], F32)
             for t in range(PACK):
                 nc.vector.bn_stats(out=stats[:, t, :], in_=h_planes[e][t])
             for t in range(PACK):
                 nc.vector.bn_aggr(out=mean_var[:, t, :], in_=stats[:, t, :])
             nc.vector.tensor_scalar_add(out=var_eps[:], in0=mean_var[:, :, 1], scalar1=EPS)
-            nc.scalar.activation(out=std[:], in_=var_eps[:], func=ACT.Sqrt)
             mean_vars[e] = mean_var
+            var_epss[e] = var_eps
+
+        def square_root(e):
+            std = small.tile([P, PACK], F32)
+            nc.scalar.activation(out=std[:], in_=var_epss[e][:], func=ACT.Sqrt)
             stds[e] = std
 
         def gain_and_shift(e):
@@ -177,49 +180,60 @@ def tile_decoder_pa_e_kernel(tc, h6_pre, g6, be6, W7_words, W7_scales, b7, out):
                     )
                 nc.scalar.copy(out=bias_all[:, e, HALF * half : HALF * (half + 1)].bitcast(F32), in_=spread[:])
 
-        def multiply(e, half):
+        def multiply(e, r, columns, result):
             plane_start = 4 * (e % SHARED)
-            result = results.tile([P, ROW_TILES, HALF], F32)
-            for c in range(HALF // N_TILE):
-                cols = slice(HALF * half + N_TILE * c, HALF * half + N_TILE * (c + 1))
-                for r in range(ROW_TILES):
-                    acc = psum_acc.tile([P, N_TILE], F32)
-                    nc.tensor.matmul_mx(
-                        out=acc[:],
-                        lhsT=a_words[:, e, P * r : P * (r + 1)].bitcast(FP8X4),
-                        lhsT_scale=a_planes[:, e, P * r : P * (r + 1)],
-                        rhs=w_words[:, e, cols].bitcast(FP8X4),
-                        rhs_scale=w_planes[plane_start:P, e // SHARED, cols],
-                        start=True,
-                        stop=True,
-                    )
-                    target = result[:, r, N_TILE * c : N_TILE * (c + 1)]
-                    if (ROW_TILES * c + r) % DETOUR_EVERY == DETOUR_EVERY - 1:
-                        nc.scalar.copy(out=target, in_=acc[:])
-                        nc.gpsimd.tensor_tensor(out=target, in0=target, in1=bias_all[:, e, cols], op=ALU.add)
-                    else:
-                        nc.vector.tensor_tensor(out=target, in0=acc[:], in1=bias_all[:, e, cols], op=ALU.add)
-            nc.sync.dma_start(
-                out=out[e].rearrange("(q r) j -> q r j", r=ROW_TILES)[:, :, HALF * half : HALF * (half + 1)], in_=result[:]
-            )
+            for c in columns:
+                cols = slice(N_TILE * c, N_TILE * (c + 1))
+                acc = psum_acc.tile([P, N_TILE], F32)
+                nc.tensor.matmul_mx(
+                    out=acc[:],
+                    lhsT=a_words[:, e, P * r : P * (r + 1)].bitcast(FP8X4),
+                    lhsT_scale=a_planes[:, e, P * r : P * (r + 1)],
+                    rhs=w_words[:, e, cols].bitcast(FP8X4),
+                    rhs_scale=w_planes[plane_start:P, e // SHARED, cols],
+                    start=True,
+                    stop=True,
+                )
+                if r == 0:
+                    nc.vector.tensor_tensor(out=result[:, cols], in0=acc[:], in1=bias_all[:, e, cols], op=ALU.add)
+                else:
+                    nc.scalar.copy(out=result[:, cols], in_=acc[:])
+
+        def add_bias(e, half, result):
+            cols = slice(HALF * half, HALF * (half + 1))
+            nc.gpsimd.tensor_tensor(out=result[:, cols], in0=result[:, cols], in1=bias_all[:, e, cols], op=ALU.add)
+
+        def store(e, r, result):
+            nc.sync.dma_start(out=out[e].rearrange("(q r) j -> q r j", r=ROW_TILES)[:, r, :], in_=result[:])
 
         for i in range(-AHEAD, BLOCKS):
-            started = i + AHEAD
-            if started < BLOCKS:
-                transpose_h(started)
-            if started == 0:
+            multiplying = i >= 0
+            quantising = 0 <= i + 1 < BLOCKS
+            norming = i + AHEAD < BLOCKS
+            if norming:
+                transpose_h(i + AHEAD)
+            if i == -AHEAD:
                 transpose_vectors()
-            if 0 <= i + 1 < BLOCKS:
+            if quantising:
                 spread_bias(i + 1)
-            if started < BLOCKS:
-                statistics(started)
-            if 0 <= i + 1 < BLOCKS:
+            if norming:
+                statistics(i + AHEAD)
+            if quantising:
                 quantise(i + 1)
-            if i >= 0:
-                multiply(i, 0)
-            if started < BLOCKS:
-                gain_and_shift(started)
-            if i >= 0:
-                multiply(i, 1)
-            if started < BLOCKS:
-                norm_and_relu(started)
+            if multiplying:
+                by_scalar = results.tile([P, COLS], F32)
+                multiply(i, 1, (0, 1), by_scalar)
+                add_bias(i, 0, by_scalar)
+            if norming:
+                square_root(i + AHEAD)
+            if multiplying:
+                multiply(i, 1, (2, 3), by_scalar)
+                add_bias(i, 1, by_scalar)
+            if norming:
+                gain_and_shift(i + AHEAD)
+                norm_and_relu(i + AHEAD)
+            if multiplying:
+                by_vector = results.tile([P, COLS], F32)
+                multiply(i, 0, (0, 1, 2, 3), by_vector)
+                store(i, 0, by_vector)
+                store(i, 1, by_scalar)

@@ -27,7 +27,7 @@ HALF = COLS // 2
 SHARED = 4
 QUADRANT = 32
 CHUNK = PAIR * P
-AHEAD = 2
+FILL = 3
 
 FLOPS = 2 * BLOCKS * ROWS * K * COLS
 
@@ -63,7 +63,7 @@ def tile_decoder_pa_e_kernel(tc, h6_pre, g6, be6, W7_words, W7_scales, b7, out):
         nc.vector.memset(w_planes[:].bitcast(I32), 0)
         nc.vector.memset(one[:], 1.0)
         make_identity(nc, identity[:])
-        nc.scalar.activation(out=warm[:], in_=one[:], func=ACT.Sqrt)
+        nc.scalar.activation(out=warm[:], in_=one[:], func=ACT.Abs_reciprocal_sqrt)
 
         def load_h(e):
             nc.sync.dma_start(out=h_rows[:, e, :, :], in_=h6_pre[e].rearrange("(q r) k -> q r k", r=ROW_TILES))
@@ -88,15 +88,14 @@ def tile_decoder_pa_e_kernel(tc, h6_pre, g6, be6, W7_words, W7_scales, b7, out):
                 )
         for e in range(BLOCKS):
             load_w(e)
-            if e + AHEAD < BLOCKS:
-                load_h(e + AHEAD)
+            if e + 2 < BLOCKS:
+                load_h(e + 2)
 
         h_planes = {}
         mean_vars = {}
-        var_epss = {}
-        stds = {}
+        rstds = {}
         scale_shifts = {}
-        a_ts = {}
+        groupeds = {}
 
         def transpose_h(e):
             h_t = psum_h.tile([P, PACK // PAIR, ROWS], F32, tag="h_t")
@@ -127,29 +126,24 @@ def tile_decoder_pa_e_kernel(tc, h6_pre, g6, be6, W7_words, W7_scales, b7, out):
         def statistics(e):
             stats = small.tile([P, PACK, 6], F32)
             mean_var = small.tile([P, PACK, 2], F32)
-            var_eps = small.tile([P, PACK], F32)
             for t in range(PACK):
                 nc.vector.bn_stats(out=stats[:, t, :], in_=h_planes[e][t])
             for t in range(PACK):
                 nc.vector.bn_aggr(out=mean_var[:, t, :], in_=stats[:, t, :])
-            nc.vector.tensor_scalar_add(out=var_eps[:], in0=mean_var[:, :, 1], scalar1=EPS)
             mean_vars[e] = mean_var
-            var_epss[e] = var_eps
 
-        def square_root(e):
-            std = small.tile([P, PACK], F32)
-            nc.scalar.activation(out=std[:], in_=var_epss[e][:], func=ACT.Sqrt)
-            stds[e] = std
+        def reciprocal_root(e):
+            rstd = small.tile([P, PACK], F32)
+            nc.scalar.activation(out=rstd[:], in_=mean_vars[e][:, :, 1], func=ACT.Abs_reciprocal_sqrt, bias=EPS)
+            rstds[e] = rstd
 
         def gain_and_shift(e):
-            rstd = small.tile([P, PACK], F32)
             scale = small.tile([P, PACK], F32)
             mean_scaled = small.tile([P, PACK], F32)
             shift = small.tile([P, PACK], F32)
-            nc.vector.reciprocal(out=rstd[:], in_=stds[e][:])
-            nc.vector.tensor_tensor(out=scale[:], in0=gain_shift[:, e, :], in1=rstd[:], op=ALU.mult)
-            nc.vector.tensor_tensor(out=mean_scaled[:], in0=mean_vars[e][:, :, 0], in1=scale[:], op=ALU.mult)
-            nc.vector.tensor_tensor(out=shift[:], in0=gain_shift[:, BLOCKS + e, :], in1=mean_scaled[:], op=ALU.subtract)
+            nc.gpsimd.tensor_tensor(out=scale[:], in0=gain_shift[:, e, :], in1=rstds[e][:], op=ALU.mult)
+            nc.gpsimd.tensor_tensor(out=mean_scaled[:], in0=mean_vars[e][:, :, 0], in1=scale[:], op=ALU.mult)
+            nc.gpsimd.tensor_tensor(out=shift[:], in0=gain_shift[:, BLOCKS + e, :], in1=mean_scaled[:], op=ALU.subtract)
             scale_shifts[e] = (scale, shift)
 
         def norm_and_relu(e):
@@ -159,15 +153,15 @@ def tile_decoder_pa_e_kernel(tc, h6_pre, g6, be6, W7_words, W7_scales, b7, out):
                 nc.scalar.activation(
                     out=a_t[:, t, :], in_=h_planes[e][t], func=ACT.Relu, scale=scale[:, t : t + 1], bias=shift[:, t : t + 1]
                 )
-            a_ts[e] = a_t
+            grouped = work.tile([P, ROWS, PACK], BF16, align_bytes=64)
+            nc.scalar.copy(out=grouped[:], in_=a_t[:].rearrange("p t n -> p n t"))
+            groupeds[e] = grouped
 
         def quantise(e):
-            grouped = work.tile([P, ROWS, PACK], BF16, align_bytes=64)
-            nc.vector.tensor_copy(out=grouped[:], in_=a_ts[e][:].rearrange("p t n -> p n t"))
             nc.vector.quantize_mx(
                 out=a_words[:, e, :].bitcast(FP8X4),
                 scales=a_planes[:, e, :],
-                in_=grouped[:].rearrange("p n t -> p (n t)"),
+                in_=groupeds[e][:].rearrange("p n t -> p (n t)"),
             )
 
         def spread_bias(e):
@@ -180,7 +174,7 @@ def tile_decoder_pa_e_kernel(tc, h6_pre, g6, be6, W7_words, W7_scales, b7, out):
                     )
                 nc.scalar.copy(out=bias_all[:, e, HALF * half : HALF * (half + 1)].bitcast(F32), in_=spread[:])
 
-        def multiply(e, r, columns, result):
+        def multiply(e, r, columns, result, by_vector):
             plane_start = 4 * (e % SHARED)
             for c in columns:
                 cols = slice(N_TILE * c, N_TILE * (c + 1))
@@ -194,46 +188,52 @@ def tile_decoder_pa_e_kernel(tc, h6_pre, g6, be6, W7_words, W7_scales, b7, out):
                     start=True,
                     stop=True,
                 )
-                if r == 0:
+                if by_vector:
                     nc.vector.tensor_tensor(out=result[:, cols], in0=acc[:], in1=bias_all[:, e, cols], op=ALU.add)
                 else:
                     nc.scalar.copy(out=result[:, cols], in_=acc[:])
 
-        def add_bias(e, half, result):
+        def add_bias(e, result):
+            nc.gpsimd.tensor_tensor(out=result[:, 0:HALF], in0=result[:, 0:HALF], in1=bias_all[:, e, 0:HALF], op=ALU.add)
+
+        def store(e, r, half, result):
             cols = slice(HALF * half, HALF * (half + 1))
-            nc.gpsimd.tensor_tensor(out=result[:, cols], in0=result[:, cols], in1=bias_all[:, e, cols], op=ALU.add)
+            nc.sync.dma_start(out=out[e].rearrange("(q r) j -> q r j", r=ROW_TILES)[:, r, cols], in_=result[:, cols])
 
-        def store(e, r, result):
-            nc.sync.dma_start(out=out[e].rearrange("(q r) j -> q r j", r=ROW_TILES)[:, r, :], in_=result[:])
+        def live(e):
+            return 0 <= e < BLOCKS
 
-        for i in range(-AHEAD, BLOCKS):
-            multiplying = i >= 0
-            quantising = 0 <= i + 1 < BLOCKS
-            norming = i + AHEAD < BLOCKS
-            if norming:
-                transpose_h(i + AHEAD)
-            if i == -AHEAD:
-                transpose_vectors()
-            if quantising:
+        for i in range(-FILL, BLOCKS):
+            detour = live(i) and live(i + 2)
+            if live(i + 2):
+                statistics(i + 2)
+            if live(i):
+                rows_1 = results.tile([P, COLS], F32)
+                multiply(i, 1, (0, 1), rows_1, not detour)
+                if not detour:
+                    store(i, 1, 0, rows_1)
+            if live(i + 2):
+                reciprocal_root(i + 2)
+                gain_and_shift(i + 2)
+            if detour:
+                add_bias(i, rows_1)
+            if live(i + 1):
+                norm_and_relu(i + 1)
+            if live(i):
+                multiply(i, 1, (2, 3), rows_1, True)
+                store(i, 1, 1, rows_1)
+                rows_0 = results.tile([P, COLS], F32)
+                multiply(i, 0, (0, 1), rows_0, True)
+                store(i, 0, 0, rows_0)
+                multiply(i, 0, (2, 3), rows_0, True)
+                store(i, 0, 1, rows_0)
+            if detour:
+                store(i, 1, 0, rows_1)
+            if live(i + 1):
                 spread_bias(i + 1)
-            if norming:
-                statistics(i + AHEAD)
-            if quantising:
+            if live(i + 3):
+                transpose_h(i + 3)
+            if i == -FILL:
+                transpose_vectors()
+            if live(i + 1):
                 quantise(i + 1)
-            if multiplying:
-                by_scalar = results.tile([P, COLS], F32)
-                multiply(i, 1, (0, 1), by_scalar)
-                add_bias(i, 0, by_scalar)
-            if norming:
-                square_root(i + AHEAD)
-            if multiplying:
-                multiply(i, 1, (2, 3), by_scalar)
-                add_bias(i, 1, by_scalar)
-            if norming:
-                gain_and_shift(i + AHEAD)
-                norm_and_relu(i + AHEAD)
-            if multiplying:
-                by_vector = results.tile([P, COLS], F32)
-                multiply(i, 0, (0, 1, 2, 3), by_vector)
-                store(i, 0, by_vector)
-                store(i, 1, by_scalar)

@@ -63,7 +63,7 @@ def tile_decoder_pa_e_kernel(tc, h6_pre, g6, be6, W7_words, W7_scales, b7, out):
         nc.vector.memset(w_planes[:].bitcast(I32), 0)
         nc.vector.memset(one[:], 1.0)
         make_identity(nc, identity[:])
-        nc.scalar.activation(out=warm[:], in_=one[:], func=ACT.Abs_reciprocal_sqrt)
+        nc.scalar.activation(out=warm[:], in_=one[:], func=ACT.Sqrt)
 
         def load_h(e):
             nc.sync.dma_start(out=h_rows[:, e, :, :], in_=h6_pre[e].rearrange("(q r) k -> q r k", r=ROW_TILES))
@@ -93,6 +93,7 @@ def tile_decoder_pa_e_kernel(tc, h6_pre, g6, be6, W7_words, W7_scales, b7, out):
 
         h_planes = {}
         mean_vars = {}
+        stds = {}
         rstds = {}
         scale_shifts = {}
         groupeds = {}
@@ -132,9 +133,14 @@ def tile_decoder_pa_e_kernel(tc, h6_pre, g6, be6, W7_words, W7_scales, b7, out):
                 nc.vector.bn_aggr(out=mean_var[:, t, :], in_=stats[:, t, :])
             mean_vars[e] = mean_var
 
-        def reciprocal_root(e):
+        def square_root(e):
+            std = small.tile([P, PACK], F32)
+            nc.scalar.activation(out=std[:], in_=mean_vars[e][:, :, 1], func=ACT.Sqrt, bias=EPS)
+            stds[e] = std
+
+        def reciprocal(e):
             rstd = small.tile([P, PACK], F32)
-            nc.scalar.activation(out=rstd[:], in_=mean_vars[e][:, :, 1], func=ACT.Abs_reciprocal_sqrt, bias=EPS)
+            nc.vector.reciprocal(out=rstd[:], in_=stds[e][:])
             rstds[e] = rstd
 
         def gain_and_shift(e):
@@ -213,15 +219,18 @@ def tile_decoder_pa_e_kernel(tc, h6_pre, g6, be6, W7_words, W7_scales, b7, out):
                 if not detour:
                     store(i, 1, 0, rows_1)
             if live(i + 2):
-                reciprocal_root(i + 2)
-                gain_and_shift(i + 2)
-            if detour:
-                add_bias(i, rows_1)
+                square_root(i + 2)
             if live(i + 1):
                 norm_and_relu(i + 1)
             if live(i):
                 multiply(i, 1, (2, 3), rows_1, True)
                 store(i, 1, 1, rows_1)
+            if live(i + 2):
+                reciprocal(i + 2)
+                gain_and_shift(i + 2)
+            if detour:
+                add_bias(i, rows_1)
+            if live(i):
                 rows_0 = results.tile([P, COLS], F32)
                 multiply(i, 0, (0, 1), rows_0, True)
                 store(i, 0, 0, rows_0)

@@ -225,15 +225,15 @@ def tile_decoder_pa_e_kernel(tc, h6_pre, g6, be6, W7_words, W7_scales, b7, out):
             if live(i):
                 multiply(i, 1, (2, 3), rows_1, True)
                 store(i, 1, 1, rows_1)
+                rows_0 = results.tile([P, COLS], F32)
+                multiply(i, 0, (0, 1), rows_0, True)
+                store(i, 0, 0, rows_0)
             if live(i + 2):
                 reciprocal(i + 2)
                 gain_and_shift(i + 2)
             if detour:
                 add_bias(i, rows_1)
             if live(i):
-                rows_0 = results.tile([P, COLS], F32)
-                multiply(i, 0, (0, 1), rows_0, True)
-                store(i, 0, 0, rows_0)
                 multiply(i, 0, (2, 3), rows_0, True)
                 store(i, 0, 1, rows_0)
             if detour:

@@ -92,6 +92,7 @@ def tile_decoder_pa_e_kernel(tc, h6_pre, g6, be6, W7_words, W7_scales, b7, out):
                 load_h(e + 2)
 
         h_planes = {}
+        h_pairs = {}
         mean_vars = {}
         stds = {}
         rstds = {}
@@ -109,6 +110,7 @@ def tile_decoder_pa_e_kernel(tc, h6_pre, g6, be6, W7_words, W7_scales, b7, out):
                     )
             pairs = h_t[:].bitcast(BF16).rearrange("p u (n i) -> p u n i", i=PAIR)
             h_planes[e] = [pairs[:, t // PAIR, :, t % PAIR] for t in range(PACK)]
+            h_pairs[e] = [h_t[:, u, :].bitcast(BF16) for u in range(PACK // PAIR)]
 
         def transpose_vectors():
             vectors_t = psum_bias.tile([P, PACK // PAIR, P], F32, tag="spread")
@@ -125,17 +127,14 @@ def tile_decoder_pa_e_kernel(tc, h6_pre, g6, be6, W7_words, W7_scales, b7, out):
             nc.vector.tensor_copy(out=bias_cols[:], in_=bias_t[:])
 
         def statistics(e):
-            stats = small.tile([P, PACK, 6], F32)
-            mean_var = small.tile([P, PACK, 2], F32)
-            for t in range(PACK):
-                nc.vector.bn_stats(out=stats[:, t, :], in_=h_planes[e][t])
-            for t in range(PACK):
-                nc.vector.bn_aggr(out=mean_var[:, t, :], in_=stats[:, t, :])
-            mean_vars[e] = mean_var
+            stats = small.tile([P, PACK // PAIR, PAIR * 3], F32)
+            for u in range(PACK // PAIR):
+                nc.vector.bn_stats(out=stats[:, u, :], in_=h_pairs[e][u])
+            mean_vars[e] = stats[:].rearrange("p u (i s) -> p (u i) s", s=3)
 
         def square_root(e):
             std = small.tile([P, PACK], F32)
-            nc.scalar.activation(out=std[:], in_=mean_vars[e][:, :, 1], func=ACT.Sqrt, bias=EPS)
+            nc.scalar.activation(out=std[:], in_=mean_vars[e][:, :, 2], func=ACT.Sqrt, scale=1.0 / ROWS, bias=EPS)
             stds[e] = std
 
         def reciprocal(e):
@@ -148,7 +147,7 @@ def tile_decoder_pa_e_kernel(tc, h6_pre, g6, be6, W7_words, W7_scales, b7, out):
             mean_scaled = small.tile([P, PACK], F32)
             shift = small.tile([P, PACK], F32)
             nc.gpsimd.tensor_tensor(out=scale[:], in0=gain_shift[:, e, :], in1=rstds[e][:], op=ALU.mult)
-            nc.gpsimd.tensor_tensor(out=mean_scaled[:], in0=mean_vars[e][:, :, 0], in1=scale[:], op=ALU.mult)
+            nc.gpsimd.tensor_tensor(out=mean_scaled[:], in0=mean_vars[e][:, :, 1], in1=scale[:], op=ALU.mult)
             nc.gpsimd.tensor_tensor(out=shift[:], in0=gain_shift[:, BLOCKS + e, :], in1=mean_scaled[:], op=ALU.subtract)
             scale_shifts[e] = (scale, shift)
 

@@ -38,7 +38,7 @@ def tile_decoder_pa_e_kernel(tc, h6_pre, g6, be6, W7_words, W7_scales, b7, out):
         keep = stack.enter_context(tc.tile_pool(name="keep", bufs=1))
         small = stack.enter_context(tc.tile_pool(name="small", bufs=2))
         work = stack.enter_context(tc.tile_pool(name="work", bufs=2))
-        results = stack.enter_context(tc.tile_pool(name="results", bufs=4))
+        results = stack.enter_context(tc.tile_pool(name="results", bufs=6))
         psum_h = stack.enter_context(tc.psum_pool(name="psum_h", bufs=2))
         psum_bias = stack.enter_context(tc.psum_pool(name="psum_bias", bufs=2))
         psum_acc = stack.enter_context(tc.psum_pool(name="psum_acc", bufs=4))
@@ -205,6 +205,9 @@ def tile_decoder_pa_e_kernel(tc, h6_pre, g6, be6, W7_words, W7_scales, b7, out):
             cols = slice(HALF * half, HALF * (half + 1))
             nc.sync.dma_start(out=out[e].rearrange("(q r) j -> q r j", r=ROW_TILES)[:, r, cols], in_=result[:, cols])
 
+        def store_block(e, both):
+            nc.sync.dma_start(out=out[e].rearrange("(q r) j -> q r j", r=ROW_TILES), in_=both[:])
+
         def live(e):
             return 0 <= e < BLOCKS
 
@@ -212,10 +215,13 @@ def tile_decoder_pa_e_kernel(tc, h6_pre, g6, be6, W7_words, W7_scales, b7, out):
             detour = live(i) and live(i + 2)
             if live(i + 2):
                 statistics(i + 2)
+            in_pieces = i == BLOCKS - 1
             if live(i):
-                rows_1 = results.tile([P, COLS], F32)
+                both = results.tile([P, ROW_TILES, COLS], F32)
+                rows_0 = both[:, 0, :]
+                rows_1 = both[:, 1, :]
                 multiply(i, 1, (0, 1), rows_1, not detour)
-                if not detour:
+                if in_pieces:
                     store(i, 1, 0, rows_1)
             if live(i + 2):
                 square_root(i + 2)
@@ -223,10 +229,11 @@ def tile_decoder_pa_e_kernel(tc, h6_pre, g6, be6, W7_words, W7_scales, b7, out):
                 norm_and_relu(i + 1)
             if live(i):
                 multiply(i, 1, (2, 3), rows_1, True)
-                store(i, 1, 1, rows_1)
-                rows_0 = results.tile([P, COLS], F32)
+                if in_pieces:
+                    store(i, 1, 1, rows_1)
                 multiply(i, 0, (0, 1), rows_0, True)
-                store(i, 0, 0, rows_0)
+                if in_pieces:
+                    store(i, 0, 0, rows_0)
             if live(i + 2):
                 reciprocal(i + 2)
                 gain_and_shift(i + 2)
@@ -234,9 +241,10 @@ def tile_decoder_pa_e_kernel(tc, h6_pre, g6, be6, W7_words, W7_scales, b7, out):
                 add_bias(i, rows_1)
             if live(i):
                 multiply(i, 0, (2, 3), rows_0, True)
-                store(i, 0, 1, rows_0)
-            if detour:
-                store(i, 1, 0, rows_1)
+                if in_pieces:
+                    store(i, 0, 1, rows_0)
+                else:
+                    store_block(i, both)
             if live(i + 1):
                 spread_bias(i + 1)
             if live(i + 3):

@@ -223,6 +223,8 @@ def tile_decoder_pa_e_kernel(tc, h6_pre, g6, be6, W7_words, W7_scales, b7, out):
                 multiply(i, 1, (0, 1), rows_1, not detour)
                 if in_pieces:
                     store(i, 1, 0, rows_1)
+            if detour:
+                add_bias(i, rows_1)
             if live(i + 2):
                 square_root(i + 2)
             if live(i + 1):
@@ -234,17 +236,14 @@ def tile_decoder_pa_e_kernel(tc, h6_pre, g6, be6, W7_words, W7_scales, b7, out):
                 multiply(i, 0, (0, 1), rows_0, True)
                 if in_pieces:
                     store(i, 0, 0, rows_0)
-            if live(i + 2):
-                reciprocal(i + 2)
-                gain_and_shift(i + 2)
-            if detour:
-                add_bias(i, rows_1)
-            if live(i):
                 multiply(i, 0, (2, 3), rows_0, True)
                 if in_pieces:
                     store(i, 0, 1, rows_0)
                 else:
                     store_block(i, both)
+            if live(i + 2):
+                reciprocal(i + 2)
+                gain_and_shift(i + 2)
             if live(i + 1):
                 spread_bias(i + 1)
             if live(i + 3):

@@ -44,8 +44,8 @@ def tile_decoder_pa_e_kernel(tc, h6_pre, g6, be6, W7_words, W7_scales, b7, out):
         psum_acc = stack.enter_context(tc.psum_pool(name="psum_acc", bufs=4))
         stack.enter_context(tc.manual_schedule())
 
-        h_rows = keep.tile([P, BLOCKS, ROW_TILES, K], BF16)
-        w_words = keep.tile([P, BLOCKS, COLS], U32, align_bytes=64)
+        h_rows = keep.tile([P, BLOCKS, ROW_TILES, K], BF16, align_bytes=256)
+        w_words = keep.tile([P, BLOCKS, COLS], U32, align_bytes=256)
         w_planes = keep.tile([P, BLOCKS // SHARED, COLS], U8, align_bytes=64)
         a_words = keep.tile([P, BLOCKS, ROWS], U32, align_bytes=64)
         a_planes = keep.tile([P, BLOCKS, ROWS], U8, align_bytes=64)
@@ -65,20 +65,25 @@ def tile_decoder_pa_e_kernel(tc, h6_pre, g6, be6, W7_words, W7_scales, b7, out):
         make_identity(nc, identity[:])
         nc.scalar.activation(out=warm[:], in_=one[:], func=ACT.Sqrt)
 
-        def load_h(e):
-            nc.sync.dma_start(out=h_rows[:, e, :, :], in_=h6_pre[e].rearrange("(q r) k -> q r k", r=ROW_TILES))
-
-        def load_w(e):
+        def load_h(first, count):
+            blocks = slice(first, first + count)
             nc.sync.dma_start(
-                out=w_words[:, e, :].bitcast(I32),
-                in_=W7_words[e].rearrange("p n t -> p (n t)").bitcast(I32),
+                out=h_rows[:, blocks, :, :].rearrange("q e r k -> q e (r k)"),
+                in_=h6_pre[blocks].rearrange("e (q r) k -> q e (r k)", r=ROW_TILES),
             )
 
-        load_h(0)
+        def load_w(first, count):
+            blocks = slice(first, first + count)
+            nc.sync.dma_start(
+                out=w_words[:, blocks, :].bitcast(I32),
+                in_=W7_words[blocks].rearrange("e p n t -> p e (n t)").bitcast(I32),
+            )
+
+        load_h(0, 1)
         nc.sync.dma_start(out=vectors[0:BLOCKS, :], in_=g6[:, :])
         nc.sync.dma_start(out=vectors[BLOCKS : 2 * BLOCKS, :], in_=be6[:, :])
         nc.sync.dma_start(out=bias_rows[0 : BLOCKS * COLS // CHUNK, :], in_=b7.rearrange("e (c j) -> (e c) j", j=CHUNK))
-        load_h(1)
+        load_h(1, 1)
         for group in range(BLOCKS // SHARED):
             for quadrant in range(P // QUADRANT):
                 first = QUADRANT * quadrant
@@ -86,10 +91,13 @@ def tile_decoder_pa_e_kernel(tc, h6_pre, g6, be6, W7_words, W7_scales, b7, out):
                     out=w_planes[first : first + 4 * SHARED, group, :].bitcast(I32),
                     in_=W7_scales[SHARED * group : SHARED * (group + 1), 4 * quadrant : 4 * quadrant + 4, :].bitcast(I32),
                 )
-        for e in range(BLOCKS):
-            load_w(e)
-            if e + 2 < BLOCKS:
-                load_h(e + 2)
+        load_w(0, 1)
+        load_h(2, 2)
+        load_w(1, 1)
+        load_w(2, 2)
+        load_h(4, 4)
+        load_w(4, 2)
+        load_w(6, 2)
 
         h_planes = {}
         h_pairs = {}
@@ -217,7 +225,7 @@ def tile_decoder_pa_e_kernel(tc, h6_pre, g6, be6, W7_words, W7_scales, b7, out):
                 statistics(i + 2)
             in_pieces = i == BLOCKS - 1
             if live(i):
-                both = results.tile([P, ROW_TILES, COLS], F32)
+                both = results.tile([P, ROW_TILES, COLS], F32, align_bytes=256)
                 rows_0 = both[:, 0, :]
                 rows_1 = both[:, 1, :]
                 multiply(i, 1, (0, 1), rows_1, not detour)

from contextlib import ExitStack

import concourse.mybir as mybir
from concourse.masks import make_identity

FP8X4 = mybir.dt.float8_e4m3fn_x4
BF16 = mybir.dt.bfloat16
F32 = mybir.dt.float32
I32 = mybir.dt.int32
U32 = mybir.dt.uint32
U8 = mybir.dt.uint8
ACT = mybir.ActivationFunctionType
ALU = mybir.AluOpType

BLOCKS = 8
ROWS = 256
K = 512
COLS = 2048
EPS = 1e-5

P = 128
PACK = 4
PAIR = 2
ROW_TILES = ROWS // P
N_TILE = 512
HALF = COLS // 2
SHARED = 4
QUADRANT = 32
CHUNK = PAIR * P
FILL = 3

FLOPS = 2 * BLOCKS * ROWS * K * COLS


def tile_decoder_pa_e_kernel(tc, h6_pre, g6, be6, W7_words, W7_scales, b7, out):
    nc = tc.nc
    with ExitStack() as stack:
        keep = stack.enter_context(tc.tile_pool(name="keep", bufs=1))
        small = stack.enter_context(tc.tile_pool(name="small", bufs=2))
        work = stack.enter_context(tc.tile_pool(name="work", bufs=2))
        results = stack.enter_context(tc.tile_pool(name="results", bufs=6))
        psum_h = stack.enter_context(tc.psum_pool(name="psum_h", bufs=2))
        psum_bias = stack.enter_context(tc.psum_pool(name="psum_bias", bufs=2))
        psum_acc = stack.enter_context(tc.psum_pool(name="psum_acc", bufs=4))
        stack.enter_context(tc.manual_schedule())

        h_rows = keep.tile([P, BLOCKS, ROW_TILES, K], BF16, align_bytes=256)
        w_words = keep.tile([P, BLOCKS, COLS], U32, align_bytes=256)
        w_planes = keep.tile([P, BLOCKS // SHARED, COLS], U8, align_bytes=64)
        a_words = keep.tile([P, BLOCKS, ROWS], U32, align_bytes=64)
        a_planes = keep.tile([P, BLOCKS, ROWS], U8, align_bytes=64)
        bias_all = keep.tile([P, BLOCKS, COLS], BF16)
        vectors = keep.tile([P, K], BF16)
        bias_rows = keep.tile([P, CHUNK], BF16)
        bias_cols = keep.tile([P, P], F32)
        gain_shift = keep.tile([P, 2 * BLOCKS, PACK], F32)
        identity = keep.tile([P, P], F32)
        one = keep.tile([P, 1], F32)
        warm = keep.tile([P, 1], F32)

        nc.vector.memset(vectors[:], 0.0)
        nc.vector.memset(bias_rows[:], 0.0)
        nc.vector.memset(w_planes[:].bitcast(I32), 0)
        nc.vector.memset(one[:], 1.0)
        make_identity(nc, identity[:])
        nc.scalar.activation(out=warm[:], in_=one[:], func=ACT.Sqrt)

        def load_h(first, count):
            blocks = slice(first, first + count)
            nc.sync.dma_start(
                out=h_rows[:, blocks, :, :].rearrange("q e r k -> q e (r k)"),
                in_=h6_pre[blocks].rearrange("e (q r) k -> q e (r k)", r=ROW_TILES),
            )

        def load_w(first, count):
            blocks = slice(first, first + count)
            nc.sync.dma_start(
                out=w_words[:, blocks, :].bitcast(I32),
                in_=W7_words[blocks].rearrange("e p n t -> p e (n t)").bitcast(I32),
            )

        load_h(0, 1)
        nc.sync.dma_start(out=vectors[0:BLOCKS, :], in_=g6[:, :])
        nc.sync.dma_start(out=vectors[BLOCKS : 2 * BLOCKS, :], in_=be6[:, :])
        nc.sync.dma_start(out=bias_rows[0 : BLOCKS * COLS // CHUNK, :], in_=b7.rearrange("e (c j) -> (e c) j", j=CHUNK))
        load_h(1, 1)
        for group in range(BLOCKS // SHARED):
            for quadrant in range(P // QUADRANT):
                first = QUADRANT * quadrant
                nc.sync.dma_start(
                    out=w_planes[first : first + 4 * SHARED, group, :].bitcast(I32),
                    in_=W7_scales[SHARED * group : SHARED * (group + 1), 4 * quadrant : 4 * quadrant + 4, :].bitcast(I32),
                )
        load_w(0, 1)
        load_h(2, 2)
        load_w(1, 1)
        load_w(2, 2)
        load_h(4, 4)
        load_w(4, 2)
        load_w(6, 2)

        h_planes = {}
        h_pairs = {}
        mean_vars = {}
        stds = {}
        rstds = {}
        scale_shifts = {}
        groupeds = {}

        def transpose_h(e):
            h_t = psum_h.tile([P, PACK // PAIR, ROWS], F32, tag="h_t")
            for r in range(ROW_TILES):
                for u in range(PACK // PAIR):
                    nc.tensor.transpose(
                        h_t[:, u, P * r : P * (r + 1)],
                        h_rows[:, e, r, :].bitcast(F32)[:, u : K // PAIR : PACK // PAIR],
                        identity[:],
                    )
            pairs = h_t[:].bitcast(BF16).rearrange("p u (n i) -> p u n i", i=PAIR)
            h_planes[e] = [pairs[:, t // PAIR, :, t % PAIR] for t in range(PACK)]
            h_pairs[e] = [h_t[:, u, :].bitcast(BF16) for u in range(PACK // PAIR)]

        def transpose_vectors():
            vectors_t = psum_bias.tile([P, PACK // PAIR, P], F32, tag="spread")
            for u in range(PACK // PAIR):
                nc.tensor.transpose(
                    vectors_t[:, u, :], vectors[:].bitcast(F32)[:, u : K // PAIR : PACK // PAIR], identity[:]
                )
            nc.vector.tensor_copy(
                out=gain_shift[:].rearrange("p v (u i) -> p v u i", i=PAIR),
                in_=vectors_t[:].bitcast(BF16).rearrange("p u (v i) -> p v u i", i=PAIR)[:, 0 : 2 * BLOCKS, :, :],
            )
            bias_t = psum_bias.tile([P, P], F32, tag="spread")
            nc.tensor.transpose(bias_t[:], bias_rows[:].bitcast(F32), identity[:])
            nc.vector.tensor_copy(out=bias_cols[:], in_=bias_t[:])

        def statistics(e):
            stats = small.tile([P, PACK // PAIR, PAIR * 3], F32)
            for u in range(PACK // PAIR):
                nc.vector.bn_stats(out=stats[:, u, :], in_=h_pairs[e][u])
            mean_vars[e] = stats[:].rearrange("p u (i s) -> p (u i) s", s=3)

        def square_root(e):
            std = small.tile([P, PACK], F32)
            nc.scalar.activation(out=std[:], in_=mean_vars[e][:, :, 2], func=ACT.Sqrt, scale=1.0 / ROWS, bias=EPS)
            stds[e] = std

        def reciprocal(e):
            rstd = small.tile([P, PACK], F32)
            nc.vector.reciprocal(out=rstd[:], in_=stds[e][:])
            rstds[e] = rstd

        def gain_and_shift(e):
            scale = small.tile([P, PACK], F32)
            mean_scaled = small.tile([P, PACK], F32)
            shift = small.tile([P, PACK], F32)
            nc.gpsimd.tensor_tensor(out=scale[:], in0=gain_shift[:, e, :], in1=rstds[e][:], op=ALU.mult)
            nc.gpsimd.tensor_tensor(out=mean_scaled[:], in0=mean_vars[e][:, :, 1], in1=scale[:], op=ALU.mult)
            nc.gpsimd.tensor_tensor(out=shift[:], in0=gain_shift[:, BLOCKS + e, :], in1=mean_scaled[:], op=ALU.subtract)
            scale_shifts[e] = (scale, shift)

        def norm_and_relu(e):
            scale, shift = scale_shifts[e]
            a_t = work.tile([P, PACK, ROWS], BF16)
            for t in range(PACK):
                nc.scalar.activation(
                    out=a_t[:, t, :], in_=h_planes[e][t], func=ACT.Relu, scale=scale[:, t : t + 1], bias=shift[:, t : t + 1]
                )
            grouped = work.tile([P, ROWS, PACK], BF16, align_bytes=64)
            nc.scalar.copy(out=grouped[:], in_=a_t[:].rearrange("p t n -> p n t"))
            groupeds[e] = grouped

        def quantise(e):
            nc.vector.quantize_mx(
                out=a_words[:, e, :].bitcast(FP8X4),
                scales=a_planes[:, e, :],
                in_=groupeds[e][:].rearrange("p n t -> p (n t)"),
            )

        def spread_bias(e):
            for half in range(COLS // HALF):
                spread = psum_bias.tile([P, N_TILE], F32, tag="spread")
                for i in range(HALF // CHUNK):
                    chunk = (COLS // CHUNK) * e + (HALF // CHUNK) * half + i
                    nc.tensor.transpose(
                        spread[:, P * i : P * (i + 1)], bias_cols[:, chunk : chunk + 1].to_broadcast([P, P]), identity[:]
                    )
                nc.scalar.copy(out=bias_all[:, e, HALF * half : HALF * (half + 1)].bitcast(F32), in_=spread[:])

        def multiply(e, r, columns, result, by_vector):
            plane_start = 4 * (e % SHARED)
            for c in columns:
                cols = slice(N_TILE * c, N_TILE * (c + 1))
                acc = psum_acc.tile([P, N_TILE], F32)
                nc.tensor.matmul_mx(
                    out=acc[:],
                    lhsT=a_words[:, e, P * r : P * (r + 1)].bitcast(FP8X4),
                    lhsT_scale=a_planes[:, e, P * r : P * (r + 1)],
                    rhs=w_words[:, e, cols].bitcast(FP8X4),
                    rhs_scale=w_planes[plane_start:P, e // SHARED, cols],
                    start=True,
                    stop=True,
                )
                if by_vector:
                    nc.vector.tensor_tensor(out=result[:, cols], in0=acc[:], in1=bias_all[:, e, cols], op=ALU.add)
                else:
                    nc.scalar.copy(out=result[:, cols], in_=acc[:])

        def add_bias(e, result):
            nc.gpsimd.tensor_tensor(out=result[:, 0:HALF], in0=result[:, 0:HALF], in1=bias_all[:, e, 0:HALF], op=ALU.add)

        def store(e, r, half, result):
            cols = slice(HALF * half, HALF * (half + 1))
            nc.sync.dma_start(out=out[e].rearrange("(q r) j -> q r j", r=ROW_TILES)[:, r, cols], in_=result[:, cols])

        def store_block(e, both):
            nc.sync.dma_start(out=out[e].rearrange("(q r) j -> q r j", r=ROW_TILES), in_=both[:])

        def live(e):
            return 0 <= e < BLOCKS

        for i in range(-FILL, BLOCKS):
            detour = live(i) and live(i + 2)
            if live(i + 2):
                statistics(i + 2)
            in_pieces = i == BLOCKS - 1
            if live(i):
                both = results.tile([P, ROW_TILES, COLS], F32, align_bytes=256)
                rows_0 = both[:, 0, :]
                rows_1 = both[:, 1, :]
                multiply(i, 1, (0, 1), rows_1, not detour)
                if in_pieces:
                    store(i, 1, 0, rows_1)
            if detour:
                add_bias(i, rows_1)
            if live(i + 2):
                square_root(i + 2)
            if live(i + 1):
                norm_and_relu(i + 1)
            if live(i):
                multiply(i, 1, (2, 3), rows_1, True)
                if in_pieces:
                    store(i, 1, 1, rows_1)
                multiply(i, 0, (0, 1), rows_0, True)
                if in_pieces:
                    store(i, 0, 0, rows_0)
                multiply(i, 0, (2, 3), rows_0, True)
                if in_pieces:
                    store(i, 0, 1, rows_0)
                else:
                    store_block(i, both)
            if live(i + 2):
                reciprocal(i + 2)
                gain_and_shift(i + 2)
            if live(i + 1):
                spread_bias(i + 1)
            if live(i + 3):
                transpose_h(i + 3)
            if i == -FILL:
                transpose_vectors()
            if live(i + 1):
                quantise(i + 1)
